import numpy as np
import ml_dtypes


def mxq(x, axis, fmt="e4m3"):
    dtype, down = {"e4m3": (ml_dtypes.float8_e4m3fn, 7), "e5m2": (ml_dtypes.float8_e5m2, 14)}[fmt]
    v = np.moveaxis(np.asarray(x, np.float32).astype(ml_dtypes.bfloat16).astype(np.float64), axis, -1)
    blocks = v.reshape(v.shape[:-1] + (-1, 32))
    amax = np.abs(blocks).max(-1, keepdims=True)
    byte = np.maximum(np.where(amax > 0, np.frexp(amax)[1] - 1 + 127, 0) - down, 1)
    scale = np.exp2(byte - 127.0)
    codes = (blocks / scale).astype(np.float32).astype(dtype).astype(np.float64)
    return np.moveaxis((codes * scale).reshape(v.shape), -1, axis)


WIDE = False


def mx_kscale(k):
    if not WIDE:
        return np.ones(k)
    levels = np.array([10, -10, 5, -5, 0])
    a = np.random.permutation(np.resize(levels, k // 512 * 4)).reshape(k // 512, 4)
    idx = np.arange(k)
    return np.exp2(a[idx // 512, idx % 128 // 32])


BF16 = ml_dtypes.bfloat16


def bf(x):
    return np.asarray(x, np.float32).astype(BF16)


def f64(x):
    return np.asarray(x).astype(np.float64)


E2M1 = np.array([0.0, 0.5, 1.0, 1.5, 2.0, 3.0, 4.0, 6.0, -0.0, -0.5, -1.0, -1.5, -2.0, -3.0, -4.0, -6.0])


def pack_weight(w, fmt):
    k, n = w.shape
    w = f64(bf(w)).reshape(k // 32, 32, n)
    amax = np.abs(w).max(1)
    if fmt == "e4m3":
        byte = np.frexp(amax)[1] - 1 + 127 - 7
    else:
        mant, ex = np.frexp(amax / 6.0)
        byte = np.where(mant > 0.5, ex, ex - 1) + 127
    byte = np.clip(np.where(amax > 0, byte, 1), 1, 254)
    scaled = (w * np.exp2(127.0 - byte)[:, None, :]).reshape(k, n).astype(np.float32)
    by_word = np.ascontiguousarray(scaled.reshape(k // 512, 128, 4, n).transpose(0, 1, 3, 2))
    if fmt == "e4m3":
        words = by_word.astype(ml_dtypes.float8_e4m3fn).view(np.uint8)
    else:
        c = by_word.astype(ml_dtypes.float4_e2m1fn).view(np.uint8) & 0xF
        words = c[..., 0::2] | (c[..., 1::2] << 4)
    return np.ascontiguousarray(words), np.ascontiguousarray(byte.astype(np.uint8).reshape(k // 512, 16, n))


def unpack_weight(words, scales, fmt):
    g, p, n, _ = words.shape
    if fmt == "e4m3":
        vals = np.ascontiguousarray(words).view(ml_dtypes.float8_e4m3fn).astype(np.float64)
    else:
        nib = np.empty((g, p, n, 4), np.uint8)
        nib[..., 0::2] = words & 0xF
        nib[..., 1::2] = words >> 4
        vals = E2M1[nib]
    vals = vals * np.repeat(np.exp2(scales.astype(np.float64) - 127.0), 8, axis=1)[..., None]
    return vals.transpose(0, 1, 3, 2).reshape(g * 512, n)

def pack4(w):
    words, scales = pack_weight(w, "e2m1")
    return words.reshape(words.shape[0], 128, -1), scales


def unpack4(words, scales):
    return unpack_weight(words.reshape(words.shape[0], 128, -1, 2), scales, "e2m1")


B, C, H, W, P = 1, 16384, 32, 16, 512
HP, WP = H // 2, W // 2
M = HP * WP
EPS = 1e-5


def maxpool2x2(x):
    return x.reshape(B, C, HP, 2, WP, 2).max(axis=(3, 5))


def setup_inputs():
    s = mx_kscale(C)
    x = bf(np.random.standard_normal((B, C, H, W)) * s[None, :, None, None])
    wk = np.random.standard_normal((P, C)) / np.sqrt(C) / s[None, :]
    wk_words, wk_scales = pack4(np.ascontiguousarray(wk.T))
    bk = bf(np.random.standard_normal(P) * 0.1)
    wv = np.random.standard_normal((P, C)) / np.sqrt(C) / s[None, :]
    wv_words, wv_scales = pack4(np.ascontiguousarray(wv.T))
    bv = bf(np.random.standard_normal(P) * 0.1)
    return {'x': x,
            'wk_words': wk_words,
            'wk_scales': wk_scales,
            'bk': bk,
            'wv_words': wv_words,
            'wv_scales': wv_scales,
            'bv': bv,
            'k_gamma': bf(np.random.uniform(0.5, 1.5, P)),
            'k_beta': bf(np.random.standard_normal(P) * 0.1),
            'k_mean': bf(np.random.standard_normal(P) * 0.1),
            'k_var': bf(np.random.uniform(0.5, 1.5, P))}


def reference(x, wk_words, wk_scales, bk, wv_words, wv_scales, bv, k_gamma, k_beta, k_mean, k_var):
    xp = mxq(maxpool2x2(f64(x)).reshape(B, C, M), 1, 'e4m3')
    k = (unpack4(wk_words, wk_scales).T @ xp) + f64(bk)[None, :, None]
    sc = f64(k_gamma) / np.sqrt(f64(k_var) + EPS)
    k = (k - f64(k_mean)[None, :, None]) * sc[None, :, None] + f64(k_beta)[None, :, None]
    v = (unpack4(wv_words, wv_scales).T @ xp) + f64(bv)[None, :, None]
    return k.reshape(B, P, HP, WP), v.reshape(B, P, HP, WP)

@@ -1,0 +1,195 @@
+from contextlib import ExitStack
+
+import concourse.mybir as mybir
+from concourse.masks import make_identity
+
+BF16 = mybir.dt.bfloat16
+F32 = mybir.dt.float32
+I32 = mybir.dt.int32
+U32 = mybir.dt.uint32
+U8 = mybir.dt.uint8
+FP8X4 = mybir.dt.float8_e4m3fn_x4
+FP4X4 = mybir.dt.float4_e2m1fn_x4
+ALU = mybir.AluOpType
+ACT = mybir.ActivationFunctionType
+
+P = 128
+PACK = 4
+C = 16384
+H, W = 32, 16
+M = (H // 2) * (W // 2)
+O = 512
+O_TILES = O // P
+PASSES = C // (P * PACK)
+EPS = 1e-5
+
+CHUNK = 2
+CHUNKS = PASSES // CHUNK
+X_LEAD = 4
+X_BUFS = 6
+SCALE_ROWS = 16
+ROWS_PER_SLOT = 4
+SCALE_SLOTS = 2 * SCALE_ROWS // ROWS_PER_SLOT
+
+FLOPS = 2 * 2 * O * C * M
+
+BK = 0
+BV = 1
+GAMMA = 2
+BETA = 3
+MEAN = 4
+VAR = 5
+
+
+def tile_nonlocalnd_bn_pa_k_kernel(
+    tc, x, wk_words, wk_scales, bk, wv_words, wv_scales, bv, k_gamma, k_beta, k_mean, k_var, out_0, out_1
+):
+    nc = tc.nc
+
+    x_chunks = x[0].rearrange("(n g p t) h w -> n p g (t h w)", g=CHUNK, p=P, t=PACK)
+    word_views = [words.bitcast(I32).rearrange("g p n -> p g n") for words in (wk_words, wv_words)]
+    scale_views = [scales.bitcast(I32) for scales in (wk_scales, wv_scales)]
+    out_views = [out[0].rearrange("(a p) h w -> p a (h w)", p=P) for out in (out_0, out_1)]
+
+    with ExitStack() as ctx:
+        keep = ctx.enter_context(tc.tile_pool(name="keep", bufs=1))
+        xin = ctx.enter_context(tc.tile_pool(name="xin", bufs=X_BUFS))
+        work = ctx.enter_context(tc.tile_pool(name="work", bufs=2))
+        psum = ctx.enter_context(tc.psum_pool(name="psum", bufs=1))
+        ctx.enter_context(tc.manual_schedule())
+
+        w_words = keep.tile([P, 2, PASSES, 2 * O], U8, align_bytes=64)
+        w_planes = keep.tile([P, 2, PASSES, O], U8, align_bytes=64)
+        x_codes = keep.tile([P, PASSES, M], U32, align_bytes=64)
+        x_planes = keep.tile([P, PASSES, M], U8, align_bytes=64)
+
+        for w in range(2):
+            nc.vector.memset(w_planes[:, w].rearrange("p g n -> p (g n)").bitcast(I32), 0)
+
+        vec_rows = keep.tile([P, P], BF16)
+        nc.gpsimd.memset(vec_rows[:], 0.0)
+        for v, vec in enumerate((bk, bv, k_gamma, k_beta, k_mean, k_var)):
+            nc.scalar.dma_start(
+                out=vec_rows[O_TILES * v : O_TILES * (v + 1), :], in_=vec.rearrange("(a c) -> a c", a=O_TILES)
+            )
+        ident = keep.tile([P, P], BF16)
+        make_identity(nc, ident[:])
+        eps = keep.tile([P, 1], F32)
+        nc.gpsimd.memset(eps[:], EPS)
+        gain = keep.tile([P, 2, O_TILES], F32)
+        nc.gpsimd.memset(gain[:], 1.0)
+        vec_cols_ps = psum.tile([P, P], BF16, tag="acc_1_3")
+        nc.tensor.transpose(out=vec_cols_ps[:], in_=vec_rows[:], identity=ident[:])
+        vec_cols = keep.tile([P, 6, O_TILES], F32)
+        nc.scalar.copy(out=vec_cols[:], in_=vec_cols_ps[:, : 6 * O_TILES].rearrange("p (v a) -> p v a", a=O_TILES))
+        std = keep.tile([P, O_TILES], F32)
+        nc.scalar.activation(out=std[:], in_=vec_cols[:, VAR, :], func=ACT.Sqrt, bias=eps[:], scale=1.0)
+
+        acc = [[psum.tile([P, M], F32, name="acc_%d_%d" % (w, a)) for a in range(O_TILES)] for w in range(2)]
+
+        x_tiles = {}
+        grouped_tiles = {}
+
+        def load_x(n):
+            xt = xin.tile([P, CHUNK, PACK * H * W], BF16)
+            nc.sync.dma_start(out=xt[:], in_=x_chunks[n])
+            x_tiles[n] = xt
+
+        scale_rows = [(w, 8 * half + i) for w in range(2) for i in range(SCALE_ROWS // 2) for half in range(2)]
+
+        def load_scale_rows(slot):
+            for w, q in scale_rows[ROWS_PER_SLOT * slot : ROWS_PER_SLOT * (slot + 1)]:
+                live = 32 * (q // 4) + q % 4
+                nc.sync.dma_start(
+                    out=w_planes[live : live + 1, w, :, :].bitcast(I32),
+                    in_=scale_views[w][:, q : q + 1, :].rearrange("g o n -> o g n"),
+                )
+
+        def load_weights(c):
+            passes = slice(CHUNK * c, CHUNK * (c + 1))
+            for w in range(2):
+                nc.sync.dma_start(out=w_words[:, w, passes, :].bitcast(I32), in_=word_views[w][:, passes, :])
+
+        def pool_chunk(c):
+            rows = x_tiles[c][:].rearrange("p g (r a w) -> p (g r) a w", a=2, w=W)
+            row_max = work.tile([P, CHUNK * PACK * M * 2], BF16)
+            nc.vector.tensor_max(
+                out=row_max[:].rearrange("p (r w) -> p r w", w=W), in0=rows[:, :, 0, :], in1=rows[:, :, 1, :]
+            )
+            pairs = row_max[:].rearrange("p (g t m b) -> p t g m b", g=CHUNK, t=PACK, b=2)
+            col_max = work.tile([P, PACK, CHUNK * M], BF16)
+            nc.vector.tensor_max(
+                out=col_max[:].rearrange("p t (g m) -> p t g m", g=CHUNK),
+                in0=pairs[:, :, :, :, 0],
+                in1=pairs[:, :, :, :, 1],
+            )
+            grouped = work.tile([P, CHUNK * M, PACK], BF16, align_bytes=64)
+            nc.scalar.copy(out=grouped[:], in_=col_max[:].rearrange("p t c -> p c t"))
+            grouped_tiles[c] = grouped
+
+        def quantise_chunk(c):
+            passes = slice(CHUNK * c, CHUNK * (c + 1))
+            nc.vector.quantize_mx(
+                out=x_codes[:, passes, :].rearrange("p g m -> p (g m)").bitcast(FP8X4),
+                scales=x_planes[:, passes, :].rearrange("p g m -> p (g m)"),
+                in_=grouped_tiles[c][:].rearrange("p c t -> p (c t)"),
+            )
+
+        def multiply_chunk(c):
+            for w in range(2):
+                for g in range(CHUNK * c, CHUNK * (c + 1)):
+                    for a in range(O_TILES):
+                        nc.tensor.matmul_mx(
+                            out=acc[w][a][:],
+                            lhsT=w_words[:, w, g, 2 * P * a : 2 * P * (a + 1)].bitcast(FP4X4),
+                            lhsT_scale=w_planes[:, w, g, P * a : P * (a + 1)],
+                            rhs=x_codes[:, g, :].bitcast(FP8X4),
+                            rhs_scale=x_planes[:, g, :],
+                            start=(g == 0),
+                            stop=(g == PASSES - 1),
+                        )
+
+        for s in range(CHUNKS + X_LEAD):
+            if s < CHUNKS:
+                load_x(s)
+            if s < SCALE_SLOTS:
+                load_scale_rows(s)
+            if s >= X_LEAD:
+                load_weights(s - X_LEAD)
+            if s < CHUNKS:
+                pool_chunk(s)
+            if 0 < s <= CHUNKS:
+                quantise_chunk(s - 1)
+
+        for c in range(CHUNKS):
+            multiply_chunk(c)
+
+        shift = keep.tile([P, 2, O_TILES], F32)
+        nc.vector.reciprocal(out=gain[:, 0, :], in_=std[:])
+        nc.vector.tensor_mul(out=gain[:, 0, :], in0=gain[:, 0, :], in1=vec_cols[:, GAMMA, :])
+        nc.vector.tensor_sub(out=shift[:, 0, :], in0=vec_cols[:, BK, :], in1=vec_cols[:, MEAN, :])
+        nc.vector.tensor_mul(out=shift[:, 0, :], in0=shift[:, 0, :], in1=gain[:, 0, :])
+        nc.vector.tensor_add(out=shift[:, 0, :], in0=shift[:, 0, :], in1=vec_cols[:, BETA, :])
+        nc.vector.tensor_copy(out=shift[:, 1, :], in_=vec_cols[:, BV, :])
+
+        result = keep.tile([P, 2, O_TILES, M], F32)
+        for w in range(2):
+            for a in range(O_TILES):
+                if a % 2 == 0:
+                    nc.vector.tensor_scalar(
+                        out=result[:, w, a, :],
+                        in0=acc[w][a][:],
+                        scalar1=gain[:, w, a : a + 1],
+                        scalar2=shift[:, w, a : a + 1],
+                        op0=ALU.mult,
+                        op1=ALU.add,
+                    )
+                else:
+                    nc.scalar.activation(
+                        out=result[:, w, a, :],
+                        in_=acc[w][a][:],
+                        func=ACT.Identity,
+                        bias=shift[:, w, a : a + 1],
+                        scale=gain[:, w, a : a + 1],
+                    )
+            nc.sync.dma_start(out=out_views[w], in_=result[:, w])

@@ -58,8 +58,8 @@ def tile_nonlocalnd_bn_pa_k_kernel(
         psum = ctx.enter_context(tc.psum_pool(name="psum", bufs=1))
         ctx.enter_context(tc.manual_schedule())
 
-        w_words = keep.tile([P, 2, PASSES, 2 * O], U8, align_bytes=64)
-        w_planes = keep.tile([P, 2, PASSES, O], U8, align_bytes=64)
+        w_words = keep.tile([P, 2, PASSES, 2 * O], U8, align_bytes=256)
+        w_planes = keep.tile([P, 2, PASSES, O], U8, align_bytes=256)
         x_codes = keep.tile([P, PASSES, M], U32, align_bytes=64)
         x_planes = keep.tile([P, PASSES, M], U8, align_bytes=64)
 
@@ -91,7 +91,7 @@ def tile_nonlocalnd_bn_pa_k_kernel(
         grouped_tiles = {}
 
         def load_x(n):
-            xt = xin.tile([P, CHUNK, PACK * H * W], BF16)
+            xt = xin.tile([P, CHUNK, PACK * H * W], BF16, align_bytes=256)
             nc.sync.dma_start(out=xt[:], in_=x_chunks[n])
             x_tiles[n] = xt
 
@@ -172,7 +172,7 @@ def tile_nonlocalnd_bn_pa_k_kernel(
         nc.vector.tensor_add(out=shift[:, 0, :], in0=shift[:, 0, :], in1=vec_cols[:, BETA, :])
         nc.vector.tensor_copy(out=shift[:, 1, :], in_=vec_cols[:, BV, :])
 
-        result = keep.tile([P, 2, O_TILES, M], F32)
+        result = keep.tile([P, 2, O_TILES, M], F32, align_bytes=256)
         for w in range(2):
             for a in range(O_TILES):
                 if a % 2 == 0:

@@ -25,8 +25,13 @@ EPS = 1e-5
 
 CHUNK = 2
 CHUNKS = PASSES // CHUNK
+X_RUNS = [(CHUNK * c, CHUNK) for c in range(CHUNKS - 1)] + [(g, 1) for g in range(PASSES - CHUNK, PASSES)]
 X_LEAD = 4
 X_BUFS = 6
+SHARED_CHUNKS = 13
+WORDS_BEHIND = {4: (0,), 5: (1,), 6: (2,), 7: (3,), 8: (4,), 9: (5,), 10: (6,), 11: (7,), 12: (8,), 13: (9,), 14: (10, 11,), 15: (12,)}
+GATHER_SLOT = CHUNKS // 4
+FOLD_SLOT = CHUNKS // 2
 SCALE_ROWS = 16
 ROWS_PER_SLOT = 4
 SCALE_SLOTS = 2 * SCALE_ROWS // ROWS_PER_SLOT
@@ -46,7 +51,7 @@ def tile_nonlocalnd_bn_pa_k_kernel(
 ):
     nc = tc.nc
 
-    x_chunks = x[0].rearrange("(n g p t) h w -> n p g (t h w)", g=CHUNK, p=P, t=PACK)
+    x_view = x[0].rearrange("(g p t) h w -> p g (t h w)", p=P, t=PACK)
     word_views = [words.bitcast(I32).rearrange("g p n -> p g n") for words in (wk_words, wv_words)]
     scale_views = [scales.bitcast(I32) for scales in (wk_scales, wv_scales)]
     out_views = [out[0].rearrange("(a p) h w -> p a (h w)", p=P) for out in (out_0, out_1)]
@@ -68,22 +73,25 @@ def tile_nonlocalnd_bn_pa_k_kernel(
 
         vec_rows = keep.tile([P, P], BF16)
         nc.gpsimd.memset(vec_rows[:], 0.0)
-        for v, vec in enumerate((bk, bv, k_gamma, k_beta, k_mean, k_var)):
-            nc.scalar.dma_start(
-                out=vec_rows[O_TILES * v : O_TILES * (v + 1), :], in_=vec.rearrange("(a c) -> a c", a=O_TILES)
-            )
         ident = keep.tile([P, P], BF16)
         make_identity(nc, ident[:])
         eps = keep.tile([P, 1], F32)
         nc.gpsimd.memset(eps[:], EPS)
         gain = keep.tile([P, 2, O_TILES], F32)
         nc.gpsimd.memset(gain[:], 1.0)
+        for v, vec in enumerate((bk, bv, k_gamma, k_beta, k_mean, k_var)):
+            nc.gpsimd.dma_start(
+                out=vec_rows[O_TILES * v : O_TILES * (v + 1), :], in_=vec.rearrange("(a c) -> a c", a=O_TILES)
+            )
         vec_cols_ps = psum.tile([P, P], BF16, tag="acc_1_3")
         nc.tensor.transpose(out=vec_cols_ps[:], in_=vec_rows[:], identity=ident[:])
         vec_cols = keep.tile([P, 6, O_TILES], F32)
-        nc.scalar.copy(out=vec_cols[:], in_=vec_cols_ps[:, : 6 * O_TILES].rearrange("p (v a) -> p v a", a=O_TILES))
         std = keep.tile([P, O_TILES], F32)
-        nc.scalar.activation(out=std[:], in_=vec_cols[:, VAR, :], func=ACT.Sqrt, bias=eps[:], scale=1.0)
+
+        def gather_vectors():
+            vec_values = vec_cols_ps[:, : 6 * O_TILES].rearrange("p (v a) -> p v a", a=O_TILES)
+            nc.scalar.copy(out=vec_cols[:], in_=vec_values)
+            nc.scalar.activation(out=std[:], in_=vec_cols[:, VAR, :], func=ACT.Sqrt, bias=eps[:], scale=1.0)
 
         acc = [[psum.tile([P, M], F32, name="acc_%d_%d" % (w, a)) for a in range(O_TILES)] for w in range(2)]
 
@@ -91,8 +99,9 @@ def tile_nonlocalnd_bn_pa_k_kernel(
         grouped_tiles = {}
 
         def load_x(n):
-            xt = xin.tile([P, CHUNK, PACK * H * W], BF16, align_bytes=256)
-            nc.sync.dma_start(out=xt[:], in_=x_chunks[n])
+            g0, count = X_RUNS[n]
+            xt = xin.tile([P, count, PACK * H * W], BF16, align_bytes=256)
+            nc.sync.dma_start(out=xt[:], in_=x_view[:, g0 : g0 + count, :])
             x_tiles[n] = xt
 
         scale_rows = [(w, 8 * half + i) for w in range(2) for i in range(SCALE_ROWS // 2) for half in range(2)]
@@ -105,75 +114,94 @@ def tile_nonlocalnd_bn_pa_k_kernel(
                     in_=scale_views[w][:, q : q + 1, :].rearrange("g o n -> o g n"),
                 )
 
-        def load_weights(c):
-            passes = slice(CHUNK * c, CHUNK * (c + 1))
-            for w in range(2):
-                nc.sync.dma_start(out=w_words[:, w, passes, :].bitcast(I32), in_=word_views[w][:, passes, :])
+        def load_words(w, g0, count):
+            passes = slice(g0, g0 + count)
+            nc.sync.dma_start(out=w_words[:, w, passes, :].bitcast(I32), in_=word_views[w][:, passes, :])
 
-        def pool_chunk(c):
-            rows = x_tiles[c][:].rearrange("p g (r a w) -> p (g r) a w", a=2, w=W)
-            row_max = work.tile([P, CHUNK * PACK * M * 2], BF16)
+        def pool_run(n):
+            count = X_RUNS[n][1]
+            rows = x_tiles[n][:].rearrange("p g (r a w) -> p (g r) a w", a=2, w=W)
+            row_max = work.tile([P, count * PACK * M * 2], BF16)
             nc.vector.tensor_max(
                 out=row_max[:].rearrange("p (r w) -> p r w", w=W), in0=rows[:, :, 0, :], in1=rows[:, :, 1, :]
             )
-            pairs = row_max[:].rearrange("p (g t m b) -> p t g m b", g=CHUNK, t=PACK, b=2)
-            col_max = work.tile([P, PACK, CHUNK * M], BF16)
+            pairs = row_max[:].rearrange("p (g t m b) -> p t g m b", g=count, t=PACK, b=2)
+            col_max = work.tile([P, PACK, count * M], BF16)
             nc.vector.tensor_max(
-                out=col_max[:].rearrange("p t (g m) -> p t g m", g=CHUNK),
+                out=col_max[:].rearrange("p t (g m) -> p t g m", g=count),
                 in0=pairs[:, :, :, :, 0],
                 in1=pairs[:, :, :, :, 1],
             )
-            grouped = work.tile([P, CHUNK * M, PACK], BF16, align_bytes=64)
+            grouped = work.tile([P, count * M, PACK], BF16, align_bytes=64)
             nc.scalar.copy(out=grouped[:], in_=col_max[:].rearrange("p t c -> p c t"))
-            grouped_tiles[c] = grouped
+            grouped_tiles[n] = grouped
 
-        def quantise_chunk(c):
-            passes = slice(CHUNK * c, CHUNK * (c + 1))
+        def quantise_run(n):
+            g0, count = X_RUNS[n]
+            passes = slice(g0, g0 + count)
             nc.vector.quantize_mx(
                 out=x_codes[:, passes, :].rearrange("p g m -> p (g m)").bitcast(FP8X4),
                 scales=x_planes[:, passes, :].rearrange("p g m -> p (g m)"),
-                in_=grouped_tiles[c][:].rearrange("p c t -> p (c t)"),
+                in_=grouped_tiles[n][:].rearrange("p c t -> p (c t)"),
             )
 
-        def multiply_chunk(c):
-            for w in range(2):
-                for g in range(CHUNK * c, CHUNK * (c + 1)):
-                    for a in range(O_TILES):
-                        nc.tensor.matmul_mx(
-                            out=acc[w][a][:],
-                            lhsT=w_words[:, w, g, 2 * P * a : 2 * P * (a + 1)].bitcast(FP4X4),
-                            lhsT_scale=w_planes[:, w, g, P * a : P * (a + 1)],
-                            rhs=x_codes[:, g, :].bitcast(FP8X4),
-                            rhs_scale=x_planes[:, g, :],
-                            start=(g == 0),
-                            stop=(g == PASSES - 1),
-                        )
-
-        for s in range(CHUNKS + X_LEAD):
-            if s < CHUNKS:
-                load_x(s)
-            if s < SCALE_SLOTS:
-                load_scale_rows(s)
-            if s >= X_LEAD:
-                load_weights(s - X_LEAD)
-            if s < CHUNKS:
-                pool_chunk(s)
-            if 0 < s <= CHUNKS:
-                quantise_chunk(s - 1)
-
-        for c in range(CHUNKS):
-            multiply_chunk(c)
+        def multiply(w, c):
+            for g in range(CHUNK * c, CHUNK * (c + 1)):
+                for a in range(O_TILES):
+                    nc.tensor.matmul_mx(
+                        out=acc[w][a][:],
+                        lhsT=w_words[:, w, g, 2 * P * a : 2 * P * (a + 1)].bitcast(FP4X4),
+                        lhsT_scale=w_planes[:, w, g, P * a : P * (a + 1)],
+                        rhs=x_codes[:, g, :].bitcast(FP8X4),
+                        rhs_scale=x_planes[:, g, :],
+                        start=(g == 0),
+                        stop=(g == PASSES - 1),
+                    )
 
         shift = keep.tile([P, 2, O_TILES], F32)
-        nc.vector.reciprocal(out=gain[:, 0, :], in_=std[:])
-        nc.vector.tensor_mul(out=gain[:, 0, :], in0=gain[:, 0, :], in1=vec_cols[:, GAMMA, :])
-        nc.vector.tensor_sub(out=shift[:, 0, :], in0=vec_cols[:, BK, :], in1=vec_cols[:, MEAN, :])
-        nc.vector.tensor_mul(out=shift[:, 0, :], in0=shift[:, 0, :], in1=gain[:, 0, :])
-        nc.vector.tensor_add(out=shift[:, 0, :], in0=shift[:, 0, :], in1=vec_cols[:, BETA, :])
-        nc.vector.tensor_copy(out=shift[:, 1, :], in_=vec_cols[:, BV, :])
 
-        result = keep.tile([P, 2, O_TILES, M], F32, align_bytes=256)
+        def fold_batch_norm():
+            nc.vector.reciprocal(out=gain[:, 0, :], in_=std[:])
+            nc.vector.tensor_mul(out=gain[:, 0, :], in0=gain[:, 0, :], in1=vec_cols[:, GAMMA, :])
+            nc.vector.tensor_sub(out=shift[:, 0, :], in0=vec_cols[:, BK, :], in1=vec_cols[:, MEAN, :])
+            nc.vector.tensor_mul(out=shift[:, 0, :], in0=shift[:, 0, :], in1=gain[:, 0, :])
+            nc.vector.tensor_add(out=shift[:, 0, :], in0=shift[:, 0, :], in1=vec_cols[:, BETA, :])
+            nc.vector.tensor_copy(out=shift[:, 1, :], in_=vec_cols[:, BV, :])
+
+        for s in range(len(X_RUNS)):
+            load_x(s)
+            if 0 < s <= SCALE_SLOTS:
+                load_scale_rows(s - 1)
+            for c in WORDS_BEHIND.get(s, ()):
+                for w in range(2):
+                    load_words(w, CHUNK * c, CHUNK)
+            pool_run(s)
+            if s > 0:
+                quantise_run(s - 1)
+            if s == GATHER_SLOT:
+                gather_vectors()
+            if s == FOLD_SLOT:
+                fold_batch_norm()
         for w in range(2):
+            for c in range(SHARED_CHUNKS, CHUNKS - w):
+                load_words(w, CHUNK * c, CHUNK)
+        for g in range(PASSES - CHUNK, PASSES):
+            load_words(1, g, 1)
+        quantise_run(len(X_RUNS) - 1)
+
+        for c in range(SHARED_CHUNKS):
+            for w in range(2):
+                multiply(w, c)
+        result = keep.tile([P, 2, O_TILES, M], F32, align_bytes=256)
+        end_passes = (
+            [(0, c) for c in range(SHARED_CHUNKS, CHUNKS - 1)]
+            + [(1, c) for c in range(SHARED_CHUNKS, CHUNKS - 2)]
+            + [(0, CHUNKS - 1)],
+            [(1, CHUNKS - 2), (1, CHUNKS - 1)],
+        )
+        for w in range(2):
+            for which, c in end_passes[w]:
+                multiply(which, c)
             for a in range(O_TILES):
                 if a % 2 == 0:
                     nc.vector.tensor_scalar(
@@ -192,4 +220,5 @@ def tile_nonlocalnd_bn_pa_k_kernel(
                         bias=shift[:, w, a : a + 1],
                         scale=gain[:, w, a : a + 1],
                     )
-            nc.sync.dma_start(out=out_views[w], in_=result[:, w])
+                if a % 2 == 1:
+                    nc.sync.dma_start(out=out_views[w][:, a - 1 : a + 1], in_=result[:, w, a - 1 : a + 1])

from contextlib import ExitStack

import concourse.mybir as mybir
from concourse.masks import make_identity

BF16 = mybir.dt.bfloat16
F32 = mybir.dt.float32
I32 = mybir.dt.int32
U32 = mybir.dt.uint32
U8 = mybir.dt.uint8
FP8X4 = mybir.dt.float8_e4m3fn_x4
FP4X4 = mybir.dt.float4_e2m1fn_x4
ALU = mybir.AluOpType
ACT = mybir.ActivationFunctionType

P = 128
PACK = 4
C = 16384
H, W = 32, 16
M = (H // 2) * (W // 2)
O = 512
O_TILES = O // P
PASSES = C // (P * PACK)
EPS = 1e-5

CHUNK = 2
CHUNKS = PASSES // CHUNK
X_RUNS = [(CHUNK * c, CHUNK) for c in range(CHUNKS - 1)] + [(g, 1) for g in range(PASSES - CHUNK, PASSES)]
X_LEAD = 4
X_BUFS = 6
SHARED_CHUNKS = 13
WORDS_BEHIND = {4: (0,), 5: (1,), 6: (2,), 7: (3,), 8: (4,), 9: (5,), 10: (6,), 11: (7,), 12: (8,), 13: (9,), 14: (10, 11,), 15: (12,)}
GATHER_SLOT = CHUNKS // 4
FOLD_SLOT = CHUNKS // 2
SCALE_ROWS = 16
ROWS_PER_SLOT = 4
SCALE_SLOTS = 2 * SCALE_ROWS // ROWS_PER_SLOT

FLOPS = 2 * 2 * O * C * M

BK = 0
BV = 1
GAMMA = 2
BETA = 3
MEAN = 4
VAR = 5


def tile_nonlocalnd_bn_pa_k_kernel(
    tc, x, wk_words, wk_scales, bk, wv_words, wv_scales, bv, k_gamma, k_beta, k_mean, k_var, out_0, out_1
):
    nc = tc.nc

    x_view = x[0].rearrange("(g p t) h w -> p g (t h w)", p=P, t=PACK)
    word_views = [words.bitcast(I32).rearrange("g p n -> p g n") for words in (wk_words, wv_words)]
    scale_views = [scales.bitcast(I32) for scales in (wk_scales, wv_scales)]
    out_views = [out[0].rearrange("(a p) h w -> p a (h w)", p=P) for out in (out_0, out_1)]

    with ExitStack() as ctx:
        keep = ctx.enter_context(tc.tile_pool(name="keep", bufs=1))
        xin = ctx.enter_context(tc.tile_pool(name="xin", bufs=X_BUFS))
        work = ctx.enter_context(tc.tile_pool(name="work", bufs=2))
        psum = ctx.enter_context(tc.psum_pool(name="psum", bufs=1))
        ctx.enter_context(tc.manual_schedule())

        w_words = keep.tile([P, 2, PASSES, 2 * O], U8, align_bytes=256)
        w_planes = keep.tile([P, 2, PASSES, O], U8, align_bytes=256)
        x_codes = keep.tile([P, PASSES, M], U32, align_bytes=64)
        x_planes = keep.tile([P, PASSES, M], U8, align_bytes=64)

        for w in range(2):
            nc.vector.memset(w_planes[:, w].rearrange("p g n -> p (g n)").bitcast(I32), 0)

        vec_rows = keep.tile([P, P], BF16)
        nc.gpsimd.memset(vec_rows[:], 0.0)
        ident = keep.tile([P, P], BF16)
        make_identity(nc, ident[:])
        eps = keep.tile([P, 1], F32)
        nc.gpsimd.memset(eps[:], EPS)
        gain = keep.tile([P, 2, O_TILES], F32)
        nc.gpsimd.memset(gain[:], 1.0)
        for v, vec in enumerate((bk, bv, k_gamma, k_beta, k_mean, k_var)):
            nc.gpsimd.dma_start(
                out=vec_rows[O_TILES * v : O_TILES * (v + 1), :], in_=vec.rearrange("(a c) -> a c", a=O_TILES)
            )
        vec_cols_ps = psum.tile([P, P], BF16, tag="acc_1_3")
        nc.tensor.transpose(out=vec_cols_ps[:], in_=vec_rows[:], identity=ident[:])
        vec_cols = keep.tile([P, 6, O_TILES], F32)
        std = keep.tile([P, O_TILES], F32)

        def gather_vectors():
            vec_values = vec_cols_ps[:, : 6 * O_TILES].rearrange("p (v a) -> p v a", a=O_TILES)
            nc.scalar.copy(out=vec_cols[:], in_=vec_values)
            nc.scalar.activation(out=std[:], in_=vec_cols[:, VAR, :], func=ACT.Sqrt, bias=eps[:], scale=1.0)

        acc = [[psum.tile([P, M], F32, name="acc_%d_%d" % (w, a)) for a in range(O_TILES)] for w in range(2)]

        x_tiles = {}
        grouped_tiles = {}

        def load_x(n):
            g0, count = X_RUNS[n]
            xt = xin.tile([P, count, PACK * H * W], BF16, align_bytes=256)
            nc.sync.dma_start(out=xt[:], in_=x_view[:, g0 : g0 + count, :])
            x_tiles[n] = xt

        scale_rows = [(w, 8 * half + i) for w in range(2) for i in range(SCALE_ROWS // 2) for half in range(2)]

        def load_scale_rows(slot):
            for w, q in scale_rows[ROWS_PER_SLOT * slot : ROWS_PER_SLOT * (slot + 1)]:
                live = 32 * (q // 4) + q % 4
                nc.sync.dma_start(
                    out=w_planes[live : live + 1, w, :, :].bitcast(I32),
                    in_=scale_views[w][:, q : q + 1, :].rearrange("g o n -> o g n"),
                )

        def load_words(w, g0, count):
            passes = slice(g0, g0 + count)
            nc.sync.dma_start(out=w_words[:, w, passes, :].bitcast(I32), in_=word_views[w][:, passes, :])

        def pool_run(n):
            count = X_RUNS[n][1]
            rows = x_tiles[n][:].rearrange("p g (r a w) -> p (g r) a w", a=2, w=W)
            row_max = work.tile([P, count * PACK * M * 2], BF16)
            nc.vector.tensor_max(
                out=row_max[:].rearrange("p (r w) -> p r w", w=W), in0=rows[:, :, 0, :], in1=rows[:, :, 1, :]
            )
            pairs = row_max[:].rearrange("p (g t m b) -> p t g m b", g=count, t=PACK, b=2)
            col_max = work.tile([P, PACK, count * M], BF16)
            nc.vector.tensor_max(
                out=col_max[:].rearrange("p t (g m) -> p t g m", g=count),
                in0=pairs[:, :, :, :, 0],
                in1=pairs[:, :, :, :, 1],
            )
            grouped = work.tile([P, count * M, PACK], BF16, align_bytes=64)
            nc.scalar.copy(out=grouped[:], in_=col_max[:].rearrange("p t c -> p c t"))
            grouped_tiles[n] = grouped

        def quantise_run(n):
            g0, count = X_RUNS[n]
            passes = slice(g0, g0 + count)
            nc.vector.quantize_mx(
                out=x_codes[:, passes, :].rearrange("p g m -> p (g m)").bitcast(FP8X4),
                scales=x_planes[:, passes, :].rearrange("p g m -> p (g m)"),
                in_=grouped_tiles[n][:].rearrange("p c t -> p (c t)"),
            )

        def multiply(w, c):
            for g in range(CHUNK * c, CHUNK * (c + 1)):
                for a in range(O_TILES):
                    nc.tensor.matmul_mx(
                        out=acc[w][a][:],
                        lhsT=w_words[:, w, g, 2 * P * a : 2 * P * (a + 1)].bitcast(FP4X4),
                        lhsT_scale=w_planes[:, w, g, P * a : P * (a + 1)],
                        rhs=x_codes[:, g, :].bitcast(FP8X4),
                        rhs_scale=x_planes[:, g, :],
                        start=(g == 0),
                        stop=(g == PASSES - 1),
                    )

        shift = keep.tile([P, 2, O_TILES], F32)

        def fold_batch_norm():
            nc.vector.reciprocal(out=gain[:, 0, :], in_=std[:])
            nc.vector.tensor_mul(out=gain[:, 0, :], in0=gain[:, 0, :], in1=vec_cols[:, GAMMA, :])
            nc.vector.tensor_sub(out=shift[:, 0, :], in0=vec_cols[:, BK, :], in1=vec_cols[:, MEAN, :])
            nc.vector.tensor_mul(out=shift[:, 0, :], in0=shift[:, 0, :], in1=gain[:, 0, :])
            nc.vector.tensor_add(out=shift[:, 0, :], in0=shift[:, 0, :], in1=vec_cols[:, BETA, :])
            nc.vector.tensor_copy(out=shift[:, 1, :], in_=vec_cols[:, BV, :])

        for s in range(len(X_RUNS)):
            load_x(s)
            if 0 < s <= SCALE_SLOTS:
                load_scale_rows(s - 1)
            for c in WORDS_BEHIND.get(s, ()):
                for w in range(2):
                    load_words(w, CHUNK * c, CHUNK)
            pool_run(s)
            if s > 0:
                quantise_run(s - 1)
            if s == GATHER_SLOT:
                gather_vectors()
            if s == FOLD_SLOT:
                fold_batch_norm()
        for w in range(2):
            for c in range(SHARED_CHUNKS, CHUNKS - w):
                load_words(w, CHUNK * c, CHUNK)
        for g in range(PASSES - CHUNK, PASSES):
            load_words(1, g, 1)
        quantise_run(len(X_RUNS) - 1)

        for c in range(SHARED_CHUNKS):
            for w in range(2):
                multiply(w, c)
        result = keep.tile([P, 2, O_TILES, M], F32, align_bytes=256)
        end_passes = (
            [(0, c) for c in range(SHARED_CHUNKS, CHUNKS - 1)]
            + [(1, c) for c in range(SHARED_CHUNKS, CHUNKS - 2)]
            + [(0, CHUNKS - 1)],
            [(1, CHUNKS - 2), (1, CHUNKS - 1)],
        )
        for w in range(2):
            for which, c in end_passes[w]:
                multiply(which, c)
            for a in range(O_TILES):
                if a % 2 == 0:
                    nc.vector.tensor_scalar(
                        out=result[:, w, a, :],
                        in0=acc[w][a][:],
                        scalar1=gain[:, w, a : a + 1],
                        scalar2=shift[:, w, a : a + 1],
                        op0=ALU.mult,
                        op1=ALU.add,
                    )
                else:
                    nc.scalar.activation(
                        out=result[:, w, a, :],
                        in_=acc[w][a][:],
                        func=ACT.Identity,
                        bias=shift[:, w, a : a + 1],
                        scale=gain[:, w, a : a + 1],
                    )
                if a % 2 == 1:
                    nc.sync.dma_start(out=out_views[w][:, a - 1 : a + 1], in_=result[:, w, a - 1 : a + 1])
